import numpy as np
import ml_dtypes


def mxq(x, axis, fmt="e4m3"):
    dtype, down = {"e4m3": (ml_dtypes.float8_e4m3fn, 7), "e5m2": (ml_dtypes.float8_e5m2, 14)}[fmt]
    v = np.moveaxis(np.asarray(x, np.float32).astype(ml_dtypes.bfloat16).astype(np.float64), axis, -1)
    blocks = v.reshape(v.shape[:-1] + (-1, 32))
    amax = np.abs(blocks).max(-1, keepdims=True)
    byte = np.maximum(np.where(amax > 0, np.frexp(amax)[1] - 1 + 127, 0) - down, 1)
    scale = np.exp2(byte - 127.0)
    codes = (blocks / scale).astype(np.float32).astype(dtype).astype(np.float64)
    return np.moveaxis((codes * scale).reshape(v.shape), -1, axis)


BF16 = ml_dtypes.bfloat16


def bf(x):
    return np.asarray(x, np.float32).astype(BF16)


def f64(x):
    return np.asarray(x).astype(np.float64)


B, S, D, R, SEG = 1, 4096, 1024, 4, 512
G = S // (R * SEG)
A = np.sqrt(np.log(SEG) + 1.5) / D ** 0.25


def setup_inputs():
    return {"x": bf(np.random.standard_normal((B, S, D)) * A)}


def reference(x):
    xs = f64(x).reshape(B, G, SEG, R, D)
    xt = np.ascontiguousarray(xs.transpose(0, 3, 1, 2, 4))
    s = (xt @ xt.transpose(0, 1, 2, 4, 3)) * (1.0 / np.sqrt(D))
    e = np.exp(s - s.max(-1, keepdims=True))
    o = (mxq(e, 4, "e4m3") @ mxq(xt, 3, "e4m3")) / e.sum(-1, keepdims=True)
    return o.transpose(0, 2, 3, 1, 4).reshape(B, S, D) / R

@@ -1,0 +1,286 @@
+from contextlib import ExitStack
+
+import concourse.mybir as mybir
+from concourse.masks import make_identity
+
+F32 = mybir.dt.float32
+BF16 = mybir.dt.bfloat16
+U32 = mybir.dt.uint32
+U8 = mybir.dt.uint8
+FP8X4 = mybir.dt.float8_e4m3fn_x4
+ACT = mybir.ActivationFunctionType
+ALU = mybir.AluOpType
+AX = mybir.AxisListType
+
+P = 128
+D = 1024
+SEG = 512
+NG = 8
+NT = 4 * NG
+FLOPS = 2 * (2 * NG * SEG * SEG * D)
+
+S_BUFS = 3
+ET_BUFS = 1
+O_BUFS = 3
+PIN = True
+
+
+def tile_dilatedattention_kernel(tc, x, out):
+    nc = tc.nc
+    xv = x.flatten_outer_dims().rearrange("(g p t r) d -> g r p t d", g=2, p=P, t=4, r=4)
+    ov = out.flatten_outer_dims().rearrange("(g p t r) d -> g r t p d", g=2, p=P, t=4, r=4)
+
+    with ExitStack() as ctx:
+        if PIN:
+            ctx.enter_context(tc.manual_schedule())
+        const = ctx.enter_context(tc.tile_pool(name="const", bufs=1))
+        xpool = ctx.enter_context(tc.tile_pool(name="xpool", bufs=1))
+        xtpool = ctx.enter_context(tc.tile_pool(name="xtpool", bufs=3))
+        xgpool = ctx.enter_context(tc.tile_pool(name="xgpool", bufs=2))
+        xqpool = ctx.enter_context(tc.tile_pool(name="xqpool", bufs=3))
+        epool = ctx.enter_context(tc.tile_pool(name="epool", bufs=3))
+        small = ctx.enter_context(tc.tile_pool(name="small", bufs=8))
+        opool = ctx.enter_context(tc.tile_pool(name="opool", bufs=6))
+        ps_s = ctx.enter_context(tc.psum_pool(name="ps_s", bufs=S_BUFS))
+        ps_xt = ctx.enter_context(tc.psum_pool(name="ps_xt", bufs=1))
+        ps_et = ctx.enter_context(tc.psum_pool(name="ps_et", bufs=ET_BUFS))
+        ps_o = ctx.enter_context(tc.psum_pool(name="ps_o", bufs=O_BUFS))
+
+        ident_f = const.tile([P, P], F32, name="ident_f")
+        ident_b = const.tile([P, P], BF16, name="ident_b")
+        make_identity(nc, ident_f[:])
+        make_identity(nc, ident_b[:])
+        warm_in = const.tile([P, 1], F32, name="warm_in")
+        warm_out = const.tile([P, 1], F32, name="warm_out")
+        nc.vector.memset(warm_in[:], 0.0)
+        nc.scalar.activation(out=warm_out[:], in_=warm_in[:], func=ACT.Exp)
+
+        x_sb = []
+        for n in range(NG):
+            xt_ = xpool.tile([P, 4 * D], BF16, name="x%d" % n)
+            x_sb.append(xt_)
+            g, r = divmod(n, 4)
+            if n == 0:
+                for t in range(4):
+                    nc.sync.dma_start(out=xt_[:, t * D:(t + 1) * D], in_=xv[g, r, :, t, :])
+            else:
+                nc.sync.dma_start(out=xt_[:].rearrange("p (t d) -> p t d", t=4), in_=xv[g, r])
+
+        xt = {}
+        xg = {}
+        xq = {}
+        xs = {}
+        st = {}
+        pend = []
+
+        def copy_on(eng, dst, src):
+            if eng == "S":
+                nc.scalar.copy(out=dst, in_=src)
+            else:
+                nc.vector.tensor_copy(out=dst, in_=src)
+
+        def xt_tile(n):
+            if n not in xt:
+                xt[n] = xtpool.tile([P, 4 * D], BF16, name="xt", tag="xt")
+            return xt[n]
+
+        def xchunk(q):
+            n, c = divmod(q, 4)
+            x32 = x_sb[n][:].bitcast(F32)
+            box = {}
+
+            def one(t):
+                if t == 0:
+                    box["ps"] = ps_xt.tile([P, 512], F32, name="xtps", tag="xtps")
+                nc.tensor.transpose(
+                    box["ps"][:, t * P:(t + 1) * P],
+                    x32[:, t * 512 + c * P:t * 512 + (c + 1) * P],
+                    ident_f[:],
+                )
+                if t == 3:
+                    pend.append((n, c, box["ps"]))
+
+            return [lambda t=t: one(t) for t in range(4)]
+
+        def flush_xt(eng):
+            for n, c, ps in list(pend):
+                dst = xt_tile(n)[:].bitcast(F32)[:, c * 512:(c + 1) * 512]
+                copy_on(eng, dst, ps[:])
+            pend[:] = []
+
+        def regroup(u):
+            n, c = divmod(u, 4)
+            if n not in xg:
+                xg[n] = xgpool.tile([P, 4 * D], BF16, name="xg", tag="xg", align_bytes=64)
+            dst = xg[n][:, c * 1024:(c + 1) * 1024].rearrange("p (c i t) -> p c t i", i=4, t=4)
+            src = x_sb[n][:].rearrange("p (t d) -> p t d", t=4)[:, :, c * 256:(c + 1) * 256]
+            nc.vector.tensor_copy(out=dst, in_=src.rearrange("p t (c i) -> p c t i", i=4))
+
+        def quant_x(u):
+            n, c = divmod(u, 4)
+            if n not in xq:
+                xq[n] = xqpool.tile([P, D], U32, name="xq", tag="xq", align_bytes=64)
+                xs[n] = xqpool.tile([P, D], U8, name="xs", tag="xs", align_bytes=64)
+            nc.vector.quantize_mx(
+                out=xq[n][:, c * 256:(c + 1) * 256].bitcast(FP8X4),
+                scales=xs[n][:, c * 256:(c + 1) * 256],
+                in_=xg[n][:, c * 1024:(c + 1) * 1024],
+            )
+
+        def mm(k, i):
+            n, tp = divmod(k, 4)
+            if i == 0:
+                st[k] = {"s": ps_s.tile([P, 512], F32, name="sps", tag="sps")}
+            c, e = divmod(i, 2)
+            v = xt[n][:].rearrange("q (c i e) -> q c i e", c=4, e=2)
+            nc.tensor.matmul(
+                st[k]["s"][:],
+                lhsT=v[:, c, tp * P:(tp + 1) * P, e],
+                rhs=v[:, c, :, e],
+                start=(i == 0),
+                stop=(i == 7),
+            )
+
+        def smax(k):
+            d = st[k]
+            d["mx"] = small.tile([P, 1], F32, name="mx", tag="mx")
+            d["nb"] = small.tile([P, 1], F32, name="nb", tag="nb")
+            nc.vector.tensor_reduce(out=d["mx"][:], in_=d["s"][:], axis=AX.X, op=ALU.max)
+            nc.vector.tensor_scalar_mul(out=d["nb"][:], in0=d["mx"][:], scalar1=-1.0 / 32.0)
+
+        def sexp(k):
+            d = st[k]
+            d["e"] = epool.tile([P, 512], BF16, name="e", tag="e")
+            d["rs"] = small.tile([P, 1], F32, name="rs", tag="rs")
+            nc.scalar.activation(
+                out=d["e"][:], in_=d["s"][:], func=ACT.Exp,
+                bias=d["nb"][:], scale=1.0 / 32.0, accum_out=d["rs"][:],
+            )
+
+        def echunk(k):
+            d = st[k]
+
+            def one(t):
+                if t == 0:
+                    d["et"] = ps_et.tile([P, 512], BF16, name="etps", tag="etps")
+                nc.tensor.transpose(
+                    d["et"][:, t * P:(t + 1) * P], d["e"][:, t * P:(t + 1) * P], ident_b[:]
+                )
+
+            return [lambda t=t: one(t) for t in range(4)]
+
+        def e_out(k, eng):
+            d = st[k]
+            d["eg"] = epool.tile([P, 512], BF16, name="eg", tag="eg", align_bytes=64)
+            copy_on(
+                eng,
+                d["eg"][:].rearrange("p (w t) -> p w t", t=4),
+                d["et"][:].rearrange("p (t w) -> p w t", t=4),
+            )
+
+        def quant_e(k):
+            d = st[k]
+            d["eq"] = epool.tile([P, P], U32, name="eq", tag="eq", align_bytes=64)
+            d["es"] = epool.tile([P, P], U8, name="es", tag="es", align_bytes=64)
+            nc.vector.quantize_mx(out=d["eq"][:].bitcast(FP8X4), scales=d["es"][:], in_=d["eg"][:])
+
+        def recip(k):
+            d = st[k]
+            d["r4"] = small.tile([P, 1], F32, name="r4", tag="r4")
+            d["rc"] = small.tile([P, 1], F32, name="rc", tag="rc")
+            nc.vector.tensor_scalar_mul(out=d["r4"][:], in0=d["rs"][:], scalar1=4.0)
+            nc.vector.reciprocal(out=d["rc"][:], in_=d["r4"][:])
+
+        def mx(k):
+            n, tp = divmod(k, 4)
+            d = st[k]
+            d["o"] = []
+            for h in range(2):
+                o_ps = ps_o.tile([P, 512], F32, name="ops", tag="ops")
+                d["o"].append(o_ps)
+                nc.tensor.matmul_mx(
+                    out=o_ps[:],
+                    lhsT=d["eq"][:].bitcast(FP8X4),
+                    lhsT_scale=d["es"][:],
+                    rhs=xq[n][:, h * 512:(h + 1) * 512].bitcast(FP8X4),
+                    rhs_scale=xs[n][:, h * 512:(h + 1) * 512],
+                    start=True,
+                    stop=True,
+                )
+
+        def oout(k):
+            n, tp = divmod(k, 4)
+            g, r = divmod(n, 4)
+            d = st[k]
+            o_sb = opool.tile([P, D], F32, name="osb", tag="osb")
+            nc.scalar.activation(out=o_sb[:, 0:512], in_=d["o"][0][:], func=ACT.Copy, scale=d["rc"][:])
+            nc.vector.tensor_scalar_mul(out=o_sb[:, 512:1024], in0=d["o"][1][:], scalar1=d["rc"][:])
+            nc.sync.dma_start(out=ov[g, r, tp], in_=o_sb[:])
+
+        x32_0 = x_sb[0][:].bitcast(F32)
+        xt32_0 = xt_tile(0)[:].bitcast(F32).rearrange("q (c t p) -> q c t p", c=4, t=4)
+        for t in range(4):
+            if t == 0:
+                ps = ps_xt.tile([P, 512], F32, name="xtps", tag="xtps")
+            else:
+                ps = ps_o.tile([P, 512], F32, name="ops", tag="ops")
+            for c in range(4):
+                nc.tensor.transpose(
+                    ps[:, c * P:(c + 1) * P],
+                    x32_0[:, t * 512 + c * P:t * 512 + (c + 1) * P],
+                    ident_f[:],
+                )
+            copy_on("S" if t % 2 == 0 else "V", xt32_0[:, :, t, :], ps[:].rearrange("q (c p) -> q c p", c=4))
+
+        def ok(k):
+            return 0 <= k < NT
+
+        next_q = [4]
+        next_rg = [0]
+        next_qx = [0]
+
+        for k in range(NT + 4):
+            if ok(k - 3):
+                quant_e(k - 3)
+            flush_xt("S")
+            if ok(k - 1):
+                smax(k - 1)
+            if ok(k - 4):
+                oout(k - 4)
+            if ok(k - 1):
+                sexp(k - 1)
+            a_list = []
+            b_list = []
+            if ok(k - 2):
+                a_list = echunk(k - 2)
+            elif k == 1:
+                a_list = xchunk(next_q[0])
+                next_q[0] += 1
+            if next_q[0] < NT and k < NT:
+                b_list = xchunk(next_q[0])
+                next_q[0] += 1
+            for i in range(5):
+                if k < NT:
+                    mm(k, i)
+                if i < 4 and a_list:
+                    a_list[i]()
+            if ok(k - 2):
+                e_out(k - 2, "S")
+            flush_xt("S")
+            if ok(k - 3):
+                mx(k - 3)
+            for i in range(5, 8):
+                if k < NT:
+                    mm(k, i)
+                if b_list:
+                    b_list[i - 5]()
+            if b_list:
+                b_list[3]()
+            while next_rg[0] < NT and next_rg[0] - 2 <= k:
+                regroup(next_rg[0])
+                next_rg[0] += 1
+            if ok(k - 2):
+                recip(k - 2)
+            while next_qx[0] < NT and next_qx[0] - 1 <= k and next_qx[0] < next_rg[0]:
+                quant_x(next_qx[0])
+                next_qx[0] += 1

@@ -19,30 +19,50 @@ NG = 8
 NT = 4 * NG
 FLOPS = 2 * (2 * NG * SEG * SEG * D)
 
-S_BUFS = 3
+S_BUFS = 2
+XT_BUFS = 2
 ET_BUFS = 1
 O_BUFS = 3
-PIN = True
+FUSED = True
+G_REGROUP = False
+MX_AFTER = 4
+XT_ENG = ("S",)
+EO_ENG = ("S",)
+XPLAN = (1, 1, 1, 1)
+OS_FIRST = True
+
+
+def tile_order():
+    seq = [(0, 0), (0, 1)]
+    for n in range(NG):
+        seq.append((n, 2))
+        if n + 1 < NG:
+            seq.append((n + 1, 0))
+        seq.append((n, 3))
+        if n + 1 < NG:
+            seq.append((n + 1, 1))
+    return seq
 
 
 def tile_dilatedattention_kernel(tc, x, out):
     nc = tc.nc
     xv = x.flatten_outer_dims().rearrange("(g p t r) d -> g r p t d", g=2, p=P, t=4, r=4)
     ov = out.flatten_outer_dims().rearrange("(g p t r) d -> g r t p d", g=2, p=P, t=4, r=4)
+    order = tile_order()
 
     with ExitStack() as ctx:
-        if PIN:
-            ctx.enter_context(tc.manual_schedule())
+        ctx.enter_context(tc.manual_schedule())
         const = ctx.enter_context(tc.tile_pool(name="const", bufs=1))
         xpool = ctx.enter_context(tc.tile_pool(name="xpool", bufs=1))
         xtpool = ctx.enter_context(tc.tile_pool(name="xtpool", bufs=3))
-        xgpool = ctx.enter_context(tc.tile_pool(name="xgpool", bufs=2))
+        xgpool = ctx.enter_context(tc.tile_pool(name="xgpool", bufs=4))
         xqpool = ctx.enter_context(tc.tile_pool(name="xqpool", bufs=3))
+        scpool = ctx.enter_context(tc.tile_pool(name="scpool", bufs=6))
         epool = ctx.enter_context(tc.tile_pool(name="epool", bufs=3))
         small = ctx.enter_context(tc.tile_pool(name="small", bufs=8))
         opool = ctx.enter_context(tc.tile_pool(name="opool", bufs=6))
         ps_s = ctx.enter_context(tc.psum_pool(name="ps_s", bufs=S_BUFS))
-        ps_xt = ctx.enter_context(tc.psum_pool(name="ps_xt", bufs=1))
+        ps_xt = ctx.enter_context(tc.psum_pool(name="ps_xt", bufs=XT_BUFS))
         ps_et = ctx.enter_context(tc.psum_pool(name="ps_et", bufs=ET_BUFS))
         ps_o = ctx.enter_context(tc.psum_pool(name="ps_o", bufs=O_BUFS))
 
@@ -70,8 +90,10 @@ def tile_dilatedattention_kernel(tc, x, out):
         xg = {}
         xq = {}
         xs = {}
+        sc = {}
         st = {}
         pend = []
+        cnt = {"xt": 0, "eo": 0}
 
         def copy_on(eng, dst, src):
             if eng == "S":
@@ -98,23 +120,36 @@ def tile_dilatedattention_kernel(tc, x, out):
                     ident_f[:],
                 )
                 if t == 3:
-                    pend.append((n, c, box["ps"]))
+                    pend.append((n, c, box["ps"], XT_ENG[cnt["xt"] % len(XT_ENG)]))
+                    cnt["xt"] += 1
 
             return [lambda t=t: one(t) for t in range(4)]
 
-        def flush_xt(eng):
-            for n, c, ps in list(pend):
-                dst = xt_tile(n)[:].bitcast(F32)[:, c * 512:(c + 1) * 512]
-                copy_on(eng, dst, ps[:])
-            pend[:] = []
+        def flush_xt(which):
+            keep = []
+            for n, c, ps, eng in list(pend):
+                if eng == which:
+                    dst = xt_tile(n)[:].bitcast(F32)[:, c * 512:(c + 1) * 512]
+                    copy_on(eng, dst, ps[:])
+                else:
+                    keep.append((n, c, ps, eng))
+            pend[:] = keep
 
-        def regroup(u):
+        def regroup(u, eng):
             n, c = divmod(u, 4)
-            if n not in xg:
-                xg[n] = xgpool.tile([P, 4 * D], BF16, name="xg", tag="xg", align_bytes=64)
-            dst = xg[n][:, c * 1024:(c + 1) * 1024].rearrange("p (c i t) -> p c t i", i=4, t=4)
+            xg[u] = xgpool.tile([P, 1024], BF16, name="xg", tag="xg", align_bytes=64)
             src = x_sb[n][:].rearrange("p (t d) -> p t d", t=4)[:, :, c * 256:(c + 1) * 256]
-            nc.vector.tensor_copy(out=dst, in_=src.rearrange("p t (c i) -> p c t i", i=4))
+            if eng == "G":
+                nc.gpsimd.tensor_scalar(
+                    out=xg[u][:].rearrange("p (d t) -> p d t", t=4),
+                    in0=src.rearrange("p t d -> p d t"),
+                    scalar1=1.0, scalar2=0.0, op0=ALU.mult, op1=ALU.add,
+                )
+            else:
+                nc.vector.tensor_copy(
+                    out=xg[u][:].rearrange("p (c i t) -> p c t i", i=4, t=4),
+                    in_=src.rearrange("p t (c i) -> p c t i", i=4),
+                )
 
         def quant_x(u):
             n, c = divmod(u, 4)
@@ -124,28 +159,49 @@ def tile_dilatedattention_kernel(tc, x, out):
             nc.vector.quantize_mx(
                 out=xq[n][:, c * 256:(c + 1) * 256].bitcast(FP8X4),
                 scales=xs[n][:, c * 256:(c + 1) * 256],
-                in_=xg[n][:, c * 1024:(c + 1) * 1024],
+                in_=xg[u][:],
             )
 
         def mm(k, i):
-            n, tp = divmod(k, 4)
+            n, tp = order[k]
             if i == 0:
                 st[k] = {"s": ps_s.tile([P, 512], F32, name="sps", tag="sps")}
             c, e = divmod(i, 2)
             v = xt[n][:].rearrange("q (c i e) -> q c i e", c=4, e=2)
             nc.tensor.matmul(
-                st[k]["s"][:],
+                st[k]["s"][:, tp * P:512],
                 lhsT=v[:, c, tp * P:(tp + 1) * P, e],
-                rhs=v[:, c, :, e],
+                rhs=v[:, c, tp * P:512, e],
                 start=(i == 0),
                 stop=(i == 7),
             )
 
+        def mirrors(k):
+            n, tp = order[k]
+            for a in range(tp):
+                nc.tensor.transpose(
+                    st[k]["s"][:, a * P:(a + 1) * P],
+                    sc[(n, a)][:, tp * P:(tp + 1) * P],
+                    ident_f[:],
+                )
+
         def smax(k):
+            n, tp = order[k]
             d = st[k]
             d["mx"] = small.tile([P, 1], F32, name="mx", tag="mx")
             d["nb"] = small.tile([P, 1], F32, name="nb", tag="nb")
-            nc.vector.tensor_reduce(out=d["mx"][:], in_=d["s"][:], axis=AX.X, op=ALU.max)
+            if tp < 3:
+                sc[(n, tp)] = scpool.tile([P, 512], F32, name="sc", tag="sc")
+            if tp < 3 and FUSED:
+                nc.vector.tensor_scalar(
+                    out=sc[(n, tp)][:], in0=d["s"][:], scalar1=1.0, scalar2=None,
+                    op0=ALU.mult, op1=ALU.max, accum_out=d["mx"][:],
+                )
+            else:
+                if tp < 3:
+                    lo = (tp + 1) * P
+                    nc.scalar.copy(out=sc[(n, tp)][:, lo:512], in_=d["s"][:, lo:512])
+                nc.vector.tensor_reduce(out=d["mx"][:], in_=d["s"][:], axis=AX.X, op=ALU.max)
             nc.vector.tensor_scalar_mul(out=d["nb"][:], in0=d["mx"][:], scalar1=-1.0 / 32.0)
 
         def sexp(k):
@@ -169,14 +225,15 @@ def tile_dilatedattention_kernel(tc, x, out):
 
             return [lambda t=t: one(t) for t in range(4)]
 
-        def e_out(k, eng):
+        def e_out(k):
             d = st[k]
             d["eg"] = epool.tile([P, 512], BF16, name="eg", tag="eg", align_bytes=64)
             copy_on(
-                eng,
+                EO_ENG[cnt["eo"] % len(EO_ENG)],
                 d["eg"][:].rearrange("p (w t) -> p w t", t=4),
                 d["et"][:].rearrange("p (t w) -> p w t", t=4),
             )
+            cnt["eo"] += 1
 
         def quant_e(k):
             d = st[k]
@@ -192,7 +249,7 @@ def tile_dilatedattention_kernel(tc, x, out):
             nc.vector.reciprocal(out=d["rc"][:], in_=d["r4"][:])
 
         def mx(k):
-            n, tp = divmod(k, 4)
+            n, tp = order[k]
             d = st[k]
             d["o"] = []
             for h in range(2):
@@ -208,19 +265,26 @@ def tile_dilatedattention_kernel(tc, x, out):
                     stop=True,
                 )
 
-        def oout(k):
-            n, tp = divmod(k, 4)
+        def oout(k, eng):
+            n, tp = order[k]
             g, r = divmod(n, 4)
             d = st[k]
-            o_sb = opool.tile([P, D], F32, name="osb", tag="osb")
-            nc.scalar.activation(out=o_sb[:, 0:512], in_=d["o"][0][:], func=ACT.Copy, scale=d["rc"][:])
-            nc.vector.tensor_scalar_mul(out=o_sb[:, 512:1024], in0=d["o"][1][:], scalar1=d["rc"][:])
-            nc.sync.dma_start(out=ov[g, r, tp], in_=o_sb[:])
+            if "osb" not in d:
+                d["osb"] = opool.tile([P, D], F32, name="osb", tag="osb")
+                d["left"] = 2
+            o_sb = d["osb"]
+            if eng == "S":
+                nc.scalar.activation(out=o_sb[:, 0:512], in_=d["o"][0][:], func=ACT.Copy, scale=d["rc"][:])
+            else:
+                nc.vector.tensor_scalar_mul(out=o_sb[:, 512:1024], in0=d["o"][1][:], scalar1=d["rc"][:])
+            d["left"] -= 1
+            if d["left"] == 0:
+                nc.sync.dma_start(out=ov[g, r, tp], in_=o_sb[:])
 
         x32_0 = x_sb[0][:].bitcast(F32)
         xt32_0 = xt_tile(0)[:].bitcast(F32).rearrange("q (c t p) -> q c t p", c=4, t=4)
         for t in range(4):
-            if t == 0:
+            if t < XT_BUFS:
                 ps = ps_xt.tile([P, 512], F32, name="xtps", tag="xtps")
             else:
                 ps = ps_o.tile([P, 512], F32, name="ops", tag="ops")
@@ -231,56 +295,68 @@ def tile_dilatedattention_kernel(tc, x, out):
                     ident_f[:],
                 )
             copy_on("S" if t % 2 == 0 else "V", xt32_0[:, :, t, :], ps[:].rearrange("q (c p) -> q c p", c=4))
+        geng = "G" if G_REGROUP else "V"
+        for u in range(4):
+            regroup(u, geng)
+        qplan = {1: [0], 2: [1], 3: [2, 3, 4]}
+        for k in range(4, NT):
+            qplan[k] = [k + 1] if k + 1 < NT else []
 
         def ok(k):
             return 0 <= k < NT
 
-        next_q = [4]
-        next_rg = [0]
-        next_qx = [0]
+        plan = {0: [4], 1: [5, 6], 2: [7]}
+        nxt = 8
+        for k in range(2, NT):
+            n, tp = order[k]
+            if k > 2:
+                plan[k] = []
+            for j in range(XPLAN[tp]):
+                if nxt < NT and k >= 4 * (nxt // 4) - 6:
+                    assert k <= 4 * (nxt // 4) - 3
+                    plan[k].append(nxt)
+                    nxt += 1
+        assert nxt == NT
 
-        for k in range(NT + 4):
-            if ok(k - 3):
-                quant_e(k - 3)
+        for k in range(NT + 5):
+            if ok(k - 4):
+                mx(k - 4)
             flush_xt("S")
             if ok(k - 1):
                 smax(k - 1)
-            if ok(k - 4):
-                oout(k - 4)
+            if ok(k - 4) and OS_FIRST:
+                oout(k - 4, "S")
             if ok(k - 1):
                 sexp(k - 1)
-            a_list = []
-            b_list = []
-            if ok(k - 2):
-                a_list = echunk(k - 2)
-            elif k == 1:
-                a_list = xchunk(next_q[0])
-                next_q[0] += 1
-            if next_q[0] < NT and k < NT:
-                b_list = xchunk(next_q[0])
-                next_q[0] += 1
-            for i in range(5):
-                if k < NT:
-                    mm(k, i)
-                if i < 4 and a_list:
-                    a_list[i]()
-            if ok(k - 2):
-                e_out(k - 2, "S")
-            flush_xt("S")
             if ok(k - 3):
-                mx(k - 3)
-            for i in range(5, 8):
-                if k < NT:
-                    mm(k, i)
-                if b_list:
-                    b_list[i - 5]()
-            if b_list:
-                b_list[3]()
-            while next_rg[0] < NT and next_rg[0] - 2 <= k:
-                regroup(next_rg[0])
-                next_rg[0] += 1
+                quant_e(k - 3)
+            for u in qplan.get(k, []):
+                quant_x(u)
+                if u + 4 < NT:
+                    regroup(u + 4, geng)
             if ok(k - 2):
                 recip(k - 2)
-            while next_qx[0] < NT and next_qx[0] - 1 <= k and next_qx[0] < next_rg[0]:
-                quant_x(next_qx[0])
-                next_qx[0] += 1
+            if ok(k - 4):
+                if not OS_FIRST:
+                    oout(k - 4, "S")
+                oout(k - 4, "V")
+            flush_xt("V")
+            e_list = echunk(k - 2) if ok(k - 2) else []
+            xl = []
+            for q in plan.get(k, []):
+                xl.extend(xchunk(q))
+            for i in range(4):
+                if k < NT:
+                    mm(k, i)
+                if e_list:
+                    e_list[i]()
+            if ok(k - 2):
+                e_out(k - 2)
+            per = len(xl) // 4
+            for i in range(4, 8):
+                if k < NT:
+                    mm(k, i)
+                for j in range(per):
+                    xl[(i - 4) * per + j]()
+            if k < NT:
+                mirrors(k)

@@ -24,7 +24,8 @@ XT_BUFS = 2
 ET_BUFS = 1
 O_BUFS = 3
 FUSED = True
-G_REGROUP = False
+G_REGROUP = True
+G_FROM = 8
 MX_AFTER = 4
 XT_ENG = ("S",)
 EO_ENG = ("S",)
@@ -295,9 +296,8 @@ def tile_dilatedattention_kernel(tc, x, out):
                     ident_f[:],
                 )
             copy_on("S" if t % 2 == 0 else "V", xt32_0[:, :, t, :], ps[:].rearrange("q (c p) -> q c p", c=4))
-        geng = "G" if G_REGROUP else "V"
         for u in range(4):
-            regroup(u, geng)
+            regroup(u, "V")
         qplan = {1: [0], 2: [1], 3: [2, 3, 4]}
         for k in range(4, NT):
             qplan[k] = [k + 1] if k + 1 < NT else []
@@ -333,7 +333,7 @@ def tile_dilatedattention_kernel(tc, x, out):
             for u in qplan.get(k, []):
                 quant_x(u)
                 if u + 4 < NT:
-                    regroup(u + 4, geng)
+                    regroup(u + 4, "G" if (G_REGROUP and u + 4 >= G_FROM) else "V")
             if ok(k - 2):
                 recip(k - 2)
             if ok(k - 4):

@@ -19,18 +19,16 @@ NG = 8
 NT = 4 * NG
 FLOPS = 2 * (2 * NG * SEG * SEG * D)
 
-S_BUFS = 2
+S_BUFS = 3
 XT_BUFS = 2
 ET_BUFS = 1
-O_BUFS = 3
-FUSED = True
-G_REGROUP = True
-G_FROM = 8
+O_BUFS = 2
+G_FROM = 4
+MX_POS = 2
 MX_AFTER = 4
 XT_ENG = ("S",)
 EO_ENG = ("S",)
 XPLAN = (1, 1, 1, 1)
-OS_FIRST = True
 
 
 def tile_order():
@@ -95,6 +93,7 @@ def tile_dilatedattention_kernel(tc, x, out):
         st = {}
         pend = []
         cnt = {"xt": 0, "eo": 0}
+        pair = {}
 
         def copy_on(eng, dst, src):
             if eng == "S":
@@ -147,9 +146,10 @@ def tile_dilatedattention_kernel(tc, x, out):
                     scalar1=1.0, scalar2=0.0, op0=ALU.mult, op1=ALU.add,
                 )
             else:
-                nc.vector.tensor_copy(
-                    out=xg[u][:].rearrange("p (c i t) -> p c t i", i=4, t=4),
-                    in_=src.rearrange("p t (c i) -> p c t i", i=4),
+                copy_on(
+                    eng,
+                    xg[u][:].rearrange("p (c i t) -> p c t i", i=4, t=4),
+                    src.rearrange("p t (c i) -> p c t i", i=4),
                 )
 
         def quant_x(u):
@@ -189,36 +189,42 @@ def tile_dilatedattention_kernel(tc, x, out):
         def smax(k):
             n, tp = order[k]
             d = st[k]
-            d["mx"] = small.tile([P, 1], F32, name="mx", tag="mx")
+            if tp < 3:
+                d["mx"] = small.tile([P, 1], F32, name="mx", tag="mx")
             d["nb"] = small.tile([P, 1], F32, name="nb", tag="nb")
             if tp < 3:
                 sc[(n, tp)] = scpool.tile([P, 512], F32, name="sc", tag="sc")
-            if tp < 3 and FUSED:
+            if tp < 3:
                 nc.vector.tensor_scalar(
                     out=sc[(n, tp)][:], in0=d["s"][:], scalar1=1.0, scalar2=None,
                     op0=ALU.mult, op1=ALU.max, accum_out=d["mx"][:],
                 )
+                nc.vector.tensor_scalar_mul(out=d["nb"][:], in0=d["mx"][:], scalar1=-1.0 / 32.0)
             else:
-                if tp < 3:
-                    lo = (tp + 1) * P
-                    nc.scalar.copy(out=sc[(n, tp)][:, lo:512], in_=d["s"][:, lo:512])
-                nc.vector.tensor_reduce(out=d["mx"][:], in_=d["s"][:], axis=AX.X, op=ALU.max)
-            nc.vector.tensor_scalar_mul(out=d["nb"][:], in0=d["mx"][:], scalar1=-1.0 / 32.0)
+                junk = scpool.tile([P, 512], F32, name="junk", tag="junk", bufs=2)
+                nc.vector.tensor_scalar(
+                    out=junk[:], in0=d["s"][:], scalar1=-1.0 / 32.0, scalar2=None,
+                    op0=ALU.mult, op1=ALU.min, accum_out=d["nb"][:],
+                )
 
         def sexp(k):
             d = st[k]
             d["e"] = epool.tile([P, 512], BF16, name="e", tag="e")
-            d["rs"] = small.tile([P, 1], F32, name="rs", tag="rs")
+            if k % 2 == 0:
+                pair["rs"] = small.tile([P, 2], F32, name="rs", tag="rs")
+            d["rs"] = pair["rs"]
             nc.scalar.activation(
                 out=d["e"][:], in_=d["s"][:], func=ACT.Exp,
-                bias=d["nb"][:], scale=1.0 / 32.0, accum_out=d["rs"][:],
+                bias=d["nb"][:], scale=1.0 / 32.0, accum_out=d["rs"][:, k % 2:k % 2 + 1],
             )
 
         def echunk(k):
             d = st[k]
 
             def one(t):
-                if t == 0:
+                if t == 0 and k == NT - 1:
+                    d["et"] = ps_s.tile([P, 512], BF16, name="sps", tag="sps")
+                elif t == 0:
                     d["et"] = ps_et.tile([P, 512], BF16, name="etps", tag="etps")
                 nc.tensor.transpose(
                     d["et"][:, t * P:(t + 1) * P], d["e"][:, t * P:(t + 1) * P], ident_b[:]
@@ -243,18 +249,24 @@ def tile_dilatedattention_kernel(tc, x, out):
             nc.vector.quantize_mx(out=d["eq"][:].bitcast(FP8X4), scales=d["es"][:], in_=d["eg"][:])
 
         def recip(k):
-            d = st[k]
-            d["r4"] = small.tile([P, 1], F32, name="r4", tag="r4")
-            d["rc"] = small.tile([P, 1], F32, name="rc", tag="rc")
-            nc.vector.tensor_scalar_mul(out=d["r4"][:], in0=d["rs"][:], scalar1=4.0)
-            nc.vector.reciprocal(out=d["rc"][:], in_=d["r4"][:])
+            r4 = small.tile([P, 2], F32, name="r4", tag="r4")
+            rc = small.tile([P, 2], F32, name="rc", tag="rc")
+            nc.vector.tensor_scalar_mul(out=r4[:], in0=st[k]["rs"][:], scalar1=4.0)
+            nc.vector.reciprocal(out=rc[:], in_=r4[:])
+            st[k - 1]["rc"] = rc[:, 0:1]
+            st[k]["rc"] = rc[:, 1:2]
 
         def mx(k):
             n, tp = order[k]
             d = st[k]
             d["o"] = []
             for h in range(2):
-                o_ps = ps_o.tile([P, 512], F32, name="ops", tag="ops")
+                if k == NT - 3:
+                    o_ps = ps_xt.tile([P, 512], F32, name="xtps", tag="xtps")
+                elif k == NT - 2:
+                    o_ps = ps_s.tile([P, 512], F32, name="sps", tag="sps")
+                else:
+                    o_ps = ps_o.tile([P, 512], F32, name="ops", tag="ops")
                 d["o"].append(o_ps)
                 nc.tensor.matmul_mx(
                     out=o_ps[:],
@@ -275,9 +287,9 @@ def tile_dilatedattention_kernel(tc, x, out):
                 d["left"] = 2
             o_sb = d["osb"]
             if eng == "S":
-                nc.scalar.activation(out=o_sb[:, 0:512], in_=d["o"][0][:], func=ACT.Copy, scale=d["rc"][:])
+                nc.scalar.activation(out=o_sb[:, 0:512], in_=d["o"][0][:], func=ACT.Copy, scale=d["rc"])
             else:
-                nc.vector.tensor_scalar_mul(out=o_sb[:, 512:1024], in0=d["o"][1][:], scalar1=d["rc"][:])
+                nc.vector.tensor_scalar_mul(out=o_sb[:, 512:1024], in0=d["o"][1][:], scalar1=d["rc"])
             d["left"] -= 1
             if d["left"] == 0:
                 nc.sync.dma_start(out=ov[g, r, tp], in_=o_sb[:])
@@ -296,10 +308,10 @@ def tile_dilatedattention_kernel(tc, x, out):
                     ident_f[:],
                 )
             copy_on("S" if t % 2 == 0 else "V", xt32_0[:, :, t, :], ps[:].rearrange("q (c p) -> q c p", c=4))
-        for u in range(4):
-            regroup(u, "V")
-        qplan = {1: [0], 2: [1], 3: [2, 3, 4]}
-        for k in range(4, NT):
+        regroup(0, "S")
+        regroup(1, "S")
+        qplan = {1: [0], 2: [1], 3: [2, 3], 4: [4], 5: [5], 6: [6, 7]}
+        for k in range(7, NT):
             qplan[k] = [k + 1] if k + 1 < NT else []
 
         def ok(k):
@@ -319,44 +331,58 @@ def tile_dilatedattention_kernel(tc, x, out):
         assert nxt == NT
 
         for k in range(NT + 5):
+            drain = k > NT
+            if drain and ok(k - 2):
+                for f in echunk(k - 2):
+                    f()
+                e_out(k - 2)
+            for i in range(MX_POS):
+                if k < NT:
+                    mm(k, i)
             if ok(k - 4):
                 mx(k - 4)
             flush_xt("S")
             if ok(k - 1):
                 smax(k - 1)
-            if ok(k - 4) and OS_FIRST:
+            if ok(k - 4) and not drain:
                 oout(k - 4, "S")
             if ok(k - 1):
                 sexp(k - 1)
+            if k in (0, 1):
+                regroup(k + 2, "S")
             if ok(k - 3):
                 quant_e(k - 3)
             for u in qplan.get(k, []):
                 quant_x(u)
                 if u + 4 < NT:
-                    regroup(u + 4, "G" if (G_REGROUP and u + 4 >= G_FROM) else "V")
-            if ok(k - 2):
+                    regroup(u + 4, "G")
+            if ok(k - 2) and (k - 2) % 2 == 1:
                 recip(k - 2)
             if ok(k - 4):
-                if not OS_FIRST:
-                    oout(k - 4, "S")
                 oout(k - 4, "V")
             flush_xt("V")
-            e_list = echunk(k - 2) if ok(k - 2) else []
+            e_list = echunk(k - 2) if (ok(k - 2) and not drain) else []
             xl = []
             for q in plan.get(k, []):
                 xl.extend(xchunk(q))
-            for i in range(4):
+            for i in range(MX_POS, 4 + MX_POS):
                 if k < NT:
                     mm(k, i)
                 if e_list:
-                    e_list[i]()
-            if ok(k - 2):
+                    e_list[i - MX_POS]()
+            if ok(k - 2) and not drain:
                 e_out(k - 2)
+            if ok(k - 4) and drain:
+                oout(k - 4, "S")
             per = len(xl) // 4
-            for i in range(4, 8):
+            rest = list(range(4 + MX_POS, 8))
+            done = 0
+            for i in rest:
                 if k < NT:
                     mm(k, i)
-                for j in range(per):
-                    xl[(i - 4) * per + j]()
+                want = (len(xl) * (i - 3 - MX_POS)) // len(rest)
+                while done < want:
+                    xl[done]()
+                    done += 1
             if k < NT:
                 mirrors(k)

@@ -20,9 +20,9 @@ NT = 4 * NG
 FLOPS = 2 * (2 * NG * SEG * SEG * D)
 
 S_BUFS = 3
-XT_BUFS = 2
+XT_BUFS = 1
 ET_BUFS = 1
-O_BUFS = 2
+O_BUFS = 3
 G_FROM = 4
 MX_POS = 2
 MX_AFTER = 4
@@ -106,13 +106,15 @@ def tile_dilatedattention_kernel(tc, x, out):
                 xt[n] = xtpool.tile([P, 4 * D], BF16, name="xt", tag="xt")
             return xt[n]
 
-        def xchunk(q):
+        def xchunk(q, spare=False):
             n, c = divmod(q, 4)
             x32 = x_sb[n][:].bitcast(F32)
             box = {}
 
             def one(t):
-                if t == 0:
+                if t == 0 and spare:
+                    box["ps"] = ps_o.tile([P, 512], F32, name="ops", tag="ops")
+                elif t == 0:
                     box["ps"] = ps_xt.tile([P, 512], F32, name="xtps", tag="xtps")
                 nc.tensor.transpose(
                     box["ps"][:, t * P:(t + 1) * P],
@@ -261,7 +263,7 @@ def tile_dilatedattention_kernel(tc, x, out):
             d = st[k]
             d["o"] = []
             for h in range(2):
-                if k == NT - 3:
+                if k == NT - 3 and h == 0:
                     o_ps = ps_xt.tile([P, 512], F32, name="xtps", tag="xtps")
                 elif k == NT - 2:
                     o_ps = ps_s.tile([P, 512], F32, name="sps", tag="sps")
@@ -308,10 +310,12 @@ def tile_dilatedattention_kernel(tc, x, out):
                     ident_f[:],
                 )
             copy_on("S" if t % 2 == 0 else "V", xt32_0[:, :, t, :], ps[:].rearrange("q (c p) -> q c p", c=4))
-        regroup(0, "S")
-        regroup(1, "S")
-        qplan = {1: [0], 2: [1], 3: [2, 3], 4: [4], 5: [5], 6: [6, 7]}
-        for k in range(7, NT):
+        for u in range(4):
+            regroup(u, "S")
+        quant_x(0)
+        regroup(4, "G")
+        qplan = {}
+        for k in range(NT):
             qplan[k] = [k + 1] if k + 1 < NT else []
 
         def ok(k):
@@ -330,12 +334,7 @@ def tile_dilatedattention_kernel(tc, x, out):
                     nxt += 1
         assert nxt == NT
 
-        for k in range(NT + 5):
-            drain = k > NT
-            if drain and ok(k - 2):
-                for f in echunk(k - 2):
-                    f()
-                e_out(k - 2)
+        for k in range(NT):
             for i in range(MX_POS):
                 if k < NT:
                     mm(k, i)
@@ -344,12 +343,10 @@ def tile_dilatedattention_kernel(tc, x, out):
             flush_xt("S")
             if ok(k - 1):
                 smax(k - 1)
-            if ok(k - 4) and not drain:
+            if ok(k - 4):
                 oout(k - 4, "S")
             if ok(k - 1):
                 sexp(k - 1)
-            if k in (0, 1):
-                regroup(k + 2, "S")
             if ok(k - 3):
                 quant_e(k - 3)
             for u in qplan.get(k, []):
@@ -358,22 +355,20 @@ def tile_dilatedattention_kernel(tc, x, out):
                     regroup(u + 4, "G")
             if ok(k - 2) and (k - 2) % 2 == 1:
                 recip(k - 2)
-            if ok(k - 4):
+            if ok(k - 4) and k < NT - 1:
                 oout(k - 4, "V")
             flush_xt("V")
-            e_list = echunk(k - 2) if (ok(k - 2) and not drain) else []
+            e_list = echunk(k - 2) if ok(k - 2) else []
             xl = []
             for q in plan.get(k, []):
-                xl.extend(xchunk(q))
+                xl.extend(xchunk(q, spare=len(xl) > 0))
             for i in range(MX_POS, 4 + MX_POS):
                 if k < NT:
                     mm(k, i)
                 if e_list:
                     e_list[i - MX_POS]()
-            if ok(k - 2) and not drain:
+            if ok(k - 2):
                 e_out(k - 2)
-            if ok(k - 4) and drain:
-                oout(k - 4, "S")
             per = len(xl) // 4
             rest = list(range(4 + MX_POS, 8))
             done = 0
@@ -386,3 +381,31 @@ def tile_dilatedattention_kernel(tc, x, out):
                     done += 1
             if k < NT:
                 mirrors(k)
+
+        def all_t(k):
+            for f in echunk(k):
+                f()
+
+        mx(NT - 4)
+        smax(NT - 1)
+        sexp(NT - 1)
+        oout(NT - 5, "V")
+        oout(NT - 4, "S")
+        quant_e(NT - 3)
+        all_t(NT - 2)
+        e_out(NT - 2)
+        oout(NT - 4, "V")
+        all_t(NT - 1)
+        e_out(NT - 1)
+        mx(NT - 3)
+        quant_e(NT - 2)
+        recip(NT - 1)
+        quant_e(NT - 1)
+        oout(NT - 3, "S")
+        oout(NT - 3, "V")
+        mx(NT - 2)
+        mx(NT - 1)
+        oout(NT - 2, "S")
+        oout(NT - 2, "V")
+        oout(NT - 1, "S")
+        oout(NT - 1, "V")

from contextlib import ExitStack

import concourse.mybir as mybir
from concourse.masks import make_identity

F32 = mybir.dt.float32
BF16 = mybir.dt.bfloat16
U32 = mybir.dt.uint32
U8 = mybir.dt.uint8
FP8X4 = mybir.dt.float8_e4m3fn_x4
ACT = mybir.ActivationFunctionType
ALU = mybir.AluOpType
AX = mybir.AxisListType

P = 128
D = 1024
SEG = 512
NG = 8
NT = 4 * NG
FLOPS = 2 * (2 * NG * SEG * SEG * D)

S_BUFS = 3
XT_BUFS = 1
ET_BUFS = 1
O_BUFS = 3
G_FROM = 4
MX_POS = 2
MX_AFTER = 4
XT_ENG = ("S",)
EO_ENG = ("S",)
XPLAN = (1, 1, 1, 1)


def tile_order():
    seq = [(0, 0), (0, 1)]
    for n in range(NG):
        seq.append((n, 2))
        if n + 1 < NG:
            seq.append((n + 1, 0))
        seq.append((n, 3))
        if n + 1 < NG:
            seq.append((n + 1, 1))
    return seq


def tile_dilatedattention_kernel(tc, x, out):
    nc = tc.nc
    xv = x.flatten_outer_dims().rearrange("(g p t r) d -> g r p t d", g=2, p=P, t=4, r=4)
    ov = out.flatten_outer_dims().rearrange("(g p t r) d -> g r t p d", g=2, p=P, t=4, r=4)
    order = tile_order()

    with ExitStack() as ctx:
        ctx.enter_context(tc.manual_schedule())
        const = ctx.enter_context(tc.tile_pool(name="const", bufs=1))
        xpool = ctx.enter_context(tc.tile_pool(name="xpool", bufs=1))
        xtpool = ctx.enter_context(tc.tile_pool(name="xtpool", bufs=3))
        xgpool = ctx.enter_context(tc.tile_pool(name="xgpool", bufs=4))
        xqpool = ctx.enter_context(tc.tile_pool(name="xqpool", bufs=3))
        scpool = ctx.enter_context(tc.tile_pool(name="scpool", bufs=6))
        epool = ctx.enter_context(tc.tile_pool(name="epool", bufs=3))
        small = ctx.enter_context(tc.tile_pool(name="small", bufs=8))
        opool = ctx.enter_context(tc.tile_pool(name="opool", bufs=6))
        ps_s = ctx.enter_context(tc.psum_pool(name="ps_s", bufs=S_BUFS))
        ps_xt = ctx.enter_context(tc.psum_pool(name="ps_xt", bufs=XT_BUFS))
        ps_et = ctx.enter_context(tc.psum_pool(name="ps_et", bufs=ET_BUFS))
        ps_o = ctx.enter_context(tc.psum_pool(name="ps_o", bufs=O_BUFS))

        ident_f = const.tile([P, P], F32, name="ident_f")
        ident_b = const.tile([P, P], BF16, name="ident_b")
        make_identity(nc, ident_f[:])
        make_identity(nc, ident_b[:])
        warm_in = const.tile([P, 1], F32, name="warm_in")
        warm_out = const.tile([P, 1], F32, name="warm_out")
        nc.vector.memset(warm_in[:], 0.0)
        nc.scalar.activation(out=warm_out[:], in_=warm_in[:], func=ACT.Exp)

        x_sb = []
        for n in range(NG):
            xt_ = xpool.tile([P, 4 * D], BF16, name="x%d" % n)
            x_sb.append(xt_)
            g, r = divmod(n, 4)
            if n == 0:
                for t in range(4):
                    nc.sync.dma_start(out=xt_[:, t * D:(t + 1) * D], in_=xv[g, r, :, t, :])
            else:
                nc.sync.dma_start(out=xt_[:].rearrange("p (t d) -> p t d", t=4), in_=xv[g, r])

        xt = {}
        xg = {}
        xq = {}
        xs = {}
        sc = {}
        st = {}
        pend = []
        cnt = {"xt": 0, "eo": 0}
        pair = {}

        def copy_on(eng, dst, src):
            if eng == "S":
                nc.scalar.copy(out=dst, in_=src)
            else:
                nc.vector.tensor_copy(out=dst, in_=src)

        def xt_tile(n):
            if n not in xt:
                xt[n] = xtpool.tile([P, 4 * D], BF16, name="xt", tag="xt")
            return xt[n]

        def xchunk(q, spare=False):
            n, c = divmod(q, 4)
            x32 = x_sb[n][:].bitcast(F32)
            box = {}

            def one(t):
                if t == 0 and spare:
                    box["ps"] = ps_o.tile([P, 512], F32, name="ops", tag="ops")
                elif t == 0:
                    box["ps"] = ps_xt.tile([P, 512], F32, name="xtps", tag="xtps")
                nc.tensor.transpose(
                    box["ps"][:, t * P:(t + 1) * P],
                    x32[:, t * 512 + c * P:t * 512 + (c + 1) * P],
                    ident_f[:],
                )
                if t == 3:
                    pend.append((n, c, box["ps"], XT_ENG[cnt["xt"] % len(XT_ENG)]))
                    cnt["xt"] += 1

            return [lambda t=t: one(t) for t in range(4)]

        def flush_xt(which):
            keep = []
            for n, c, ps, eng in list(pend):
                if eng == which:
                    dst = xt_tile(n)[:].bitcast(F32)[:, c * 512:(c + 1) * 512]
                    copy_on(eng, dst, ps[:])
                else:
                    keep.append((n, c, ps, eng))
            pend[:] = keep

        def regroup(u, eng):
            n, c = divmod(u, 4)
            xg[u] = xgpool.tile([P, 1024], BF16, name="xg", tag="xg", align_bytes=64)
            src = x_sb[n][:].rearrange("p (t d) -> p t d", t=4)[:, :, c * 256:(c + 1) * 256]
            if eng == "G":
                nc.gpsimd.tensor_scalar(
                    out=xg[u][:].rearrange("p (d t) -> p d t", t=4),
                    in0=src.rearrange("p t d -> p d t"),
                    scalar1=1.0, scalar2=0.0, op0=ALU.mult, op1=ALU.add,
                )
            else:
                copy_on(
                    eng,
                    xg[u][:].rearrange("p (c i t) -> p c t i", i=4, t=4),
                    src.rearrange("p t (c i) -> p c t i", i=4),
                )

        def quant_x(u):
            n, c = divmod(u, 4)
            if n not in xq:
                xq[n] = xqpool.tile([P, D], U32, name="xq", tag="xq", align_bytes=64)
                xs[n] = xqpool.tile([P, D], U8, name="xs", tag="xs", align_bytes=64)
            nc.vector.quantize_mx(
                out=xq[n][:, c * 256:(c + 1) * 256].bitcast(FP8X4),
                scales=xs[n][:, c * 256:(c + 1) * 256],
                in_=xg[u][:],
            )

        def mm(k, i):
            n, tp = order[k]
            if i == 0:
                st[k] = {"s": ps_s.tile([P, 512], F32, name="sps", tag="sps")}
            c, e = divmod(i, 2)
            v = xt[n][:].rearrange("q (c i e) -> q c i e", c=4, e=2)
            nc.tensor.matmul(
                st[k]["s"][:, tp * P:512],
                lhsT=v[:, c, tp * P:(tp + 1) * P, e],
                rhs=v[:, c, tp * P:512, e],
                start=(i == 0),
                stop=(i == 7),
            )

        def mirrors(k):
            n, tp = order[k]
            for a in range(tp):
                nc.tensor.transpose(
                    st[k]["s"][:, a * P:(a + 1) * P],
                    sc[(n, a)][:, tp * P:(tp + 1) * P],
                    ident_f[:],
                )

        def smax(k):
            n, tp = order[k]
            d = st[k]
            if tp < 3:
                d["mx"] = small.tile([P, 1], F32, name="mx", tag="mx")
            d["nb"] = small.tile([P, 1], F32, name="nb", tag="nb")
            if tp < 3:
                sc[(n, tp)] = scpool.tile([P, 512], F32, name="sc", tag="sc")
            if tp < 3:
                nc.vector.tensor_scalar(
                    out=sc[(n, tp)][:], in0=d["s"][:], scalar1=1.0, scalar2=None,
                    op0=ALU.mult, op1=ALU.max, accum_out=d["mx"][:],
                )
                nc.vector.tensor_scalar_mul(out=d["nb"][:], in0=d["mx"][:], scalar1=-1.0 / 32.0)
            else:
                junk = scpool.tile([P, 512], F32, name="junk", tag="junk", bufs=2)
                nc.vector.tensor_scalar(
                    out=junk[:], in0=d["s"][:], scalar1=-1.0 / 32.0, scalar2=None,
                    op0=ALU.mult, op1=ALU.min, accum_out=d["nb"][:],
                )

        def sexp(k):
            d = st[k]
            d["e"] = epool.tile([P, 512], BF16, name="e", tag="e")
            if k % 2 == 0:
                pair["rs"] = small.tile([P, 2], F32, name="rs", tag="rs")
            d["rs"] = pair["rs"]
            nc.scalar.activation(
                out=d["e"][:], in_=d["s"][:], func=ACT.Exp,
                bias=d["nb"][:], scale=1.0 / 32.0, accum_out=d["rs"][:, k % 2:k % 2 + 1],
            )

        def echunk(k):
            d = st[k]

            def one(t):
                if t == 0 and k == NT - 1:
                    d["et"] = ps_s.tile([P, 512], BF16, name="sps", tag="sps")
                elif t == 0:
                    d["et"] = ps_et.tile([P, 512], BF16, name="etps", tag="etps")
                nc.tensor.transpose(
                    d["et"][:, t * P:(t + 1) * P], d["e"][:, t * P:(t + 1) * P], ident_b[:]
                )

            return [lambda t=t: one(t) for t in range(4)]

        def e_out(k):
            d = st[k]
            d["eg"] = epool.tile([P, 512], BF16, name="eg", tag="eg", align_bytes=64)
            copy_on(
                EO_ENG[cnt["eo"] % len(EO_ENG)],
                d["eg"][:].rearrange("p (w t) -> p w t", t=4),
                d["et"][:].rearrange("p (t w) -> p w t", t=4),
            )
            cnt["eo"] += 1

        def quant_e(k):
            d = st[k]
            d["eq"] = epool.tile([P, P], U32, name="eq", tag="eq", align_bytes=64)
            d["es"] = epool.tile([P, P], U8, name="es", tag="es", align_bytes=64)
            nc.vector.quantize_mx(out=d["eq"][:].bitcast(FP8X4), scales=d["es"][:], in_=d["eg"][:])

        def recip(k):
            r4 = small.tile([P, 2], F32, name="r4", tag="r4")
            rc = small.tile([P, 2], F32, name="rc", tag="rc")
            nc.vector.tensor_scalar_mul(out=r4[:], in0=st[k]["rs"][:], scalar1=4.0)
            nc.vector.reciprocal(out=rc[:], in_=r4[:])
            st[k - 1]["rc"] = rc[:, 0:1]
            st[k]["rc"] = rc[:, 1:2]

        def mx(k):
            n, tp = order[k]
            d = st[k]
            d["o"] = []
            for h in range(2):
                if k == NT - 3 and h == 0:
                    o_ps = ps_xt.tile([P, 512], F32, name="xtps", tag="xtps")
                elif k == NT - 2:
                    o_ps = ps_s.tile([P, 512], F32, name="sps", tag="sps")
                else:
                    o_ps = ps_o.tile([P, 512], F32, name="ops", tag="ops")
                d["o"].append(o_ps)
                nc.tensor.matmul_mx(
                    out=o_ps[:],
                    lhsT=d["eq"][:].bitcast(FP8X4),
                    lhsT_scale=d["es"][:],
                    rhs=xq[n][:, h * 512:(h + 1) * 512].bitcast(FP8X4),
                    rhs_scale=xs[n][:, h * 512:(h + 1) * 512],
                    start=True,
                    stop=True,
                )

        def oout(k, eng):
            n, tp = order[k]
            g, r = divmod(n, 4)
            d = st[k]
            if "osb" not in d:
                d["osb"] = opool.tile([P, D], F32, name="osb", tag="osb")
                d["left"] = 2
            o_sb = d["osb"]
            if eng == "S":
                nc.scalar.activation(out=o_sb[:, 0:512], in_=d["o"][0][:], func=ACT.Copy, scale=d["rc"])
            else:
                nc.vector.tensor_scalar_mul(out=o_sb[:, 512:1024], in0=d["o"][1][:], scalar1=d["rc"])
            d["left"] -= 1
            if d["left"] == 0:
                nc.sync.dma_start(out=ov[g, r, tp], in_=o_sb[:])

        x32_0 = x_sb[0][:].bitcast(F32)
        xt32_0 = xt_tile(0)[:].bitcast(F32).rearrange("q (c t p) -> q c t p", c=4, t=4)
        for t in range(4):
            if t < XT_BUFS:
                ps = ps_xt.tile([P, 512], F32, name="xtps", tag="xtps")
            else:
                ps = ps_o.tile([P, 512], F32, name="ops", tag="ops")
            for c in range(4):
                nc.tensor.transpose(
                    ps[:, c * P:(c + 1) * P],
                    x32_0[:, t * 512 + c * P:t * 512 + (c + 1) * P],
                    ident_f[:],
                )
            copy_on("S" if t % 2 == 0 else "V", xt32_0[:, :, t, :], ps[:].rearrange("q (c p) -> q c p", c=4))
        for u in range(4):
            regroup(u, "S")
        quant_x(0)
        regroup(4, "G")
        qplan = {}
        for k in range(NT):
            qplan[k] = [k + 1] if k + 1 < NT else []

        def ok(k):
            return 0 <= k < NT

        plan = {0: [4], 1: [5, 6], 2: [7]}
        nxt = 8
        for k in range(2, NT):
            n, tp = order[k]
            if k > 2:
                plan[k] = []
            for j in range(XPLAN[tp]):
                if nxt < NT and k >= 4 * (nxt // 4) - 6:
                    assert k <= 4 * (nxt // 4) - 3
                    plan[k].append(nxt)
                    nxt += 1
        assert nxt == NT

        for k in range(NT):
            for i in range(MX_POS):
                if k < NT:
                    mm(k, i)
            if ok(k - 4):
                mx(k - 4)
            flush_xt("S")
            if ok(k - 1):
                smax(k - 1)
            if ok(k - 4):
                oout(k - 4, "S")
            if ok(k - 1):
                sexp(k - 1)
            if ok(k - 3):
                quant_e(k - 3)
            for u in qplan.get(k, []):
                quant_x(u)
                if u + 4 < NT:
                    regroup(u + 4, "G")
            if ok(k - 2) and (k - 2) % 2 == 1:
                recip(k - 2)
            if ok(k - 4) and k < NT - 1:
                oout(k - 4, "V")
            flush_xt("V")
            e_list = echunk(k - 2) if ok(k - 2) else []
            xl = []
            for q in plan.get(k, []):
                xl.extend(xchunk(q, spare=len(xl) > 0))
            for i in range(MX_POS, 4 + MX_POS):
                if k < NT:
                    mm(k, i)
                if e_list:
                    e_list[i - MX_POS]()
            if ok(k - 2):
                e_out(k - 2)
            per = len(xl) // 4
            rest = list(range(4 + MX_POS, 8))
            done = 0
            for i in rest:
                if k < NT:
                    mm(k, i)
                want = (len(xl) * (i - 3 - MX_POS)) // len(rest)
                while done < want:
                    xl[done]()
                    done += 1
            if k < NT:
                mirrors(k)

        def all_t(k):
            for f in echunk(k):
                f()

        mx(NT - 4)
        smax(NT - 1)
        sexp(NT - 1)
        oout(NT - 5, "V")
        oout(NT - 4, "S")
        quant_e(NT - 3)
        all_t(NT - 2)
        e_out(NT - 2)
        oout(NT - 4, "V")
        all_t(NT - 1)
        e_out(NT - 1)
        mx(NT - 3)
        quant_e(NT - 2)
        recip(NT - 1)
        quant_e(NT - 1)
        oout(NT - 3, "S")
        oout(NT - 3, "V")
        mx(NT - 2)
        mx(NT - 1)
        oout(NT - 2, "S")
        oout(NT - 2, "V")
        oout(NT - 1, "S")
        oout(NT - 1, "V")
